import numpy as np
import ml_dtypes


def mxq(x, axis, fmt="e4m3"):
    dtype, down = {"e4m3": (ml_dtypes.float8_e4m3fn, 7), "e5m2": (ml_dtypes.float8_e5m2, 14)}[fmt]
    v = np.moveaxis(np.asarray(x, np.float32).astype(ml_dtypes.bfloat16).astype(np.float64), axis, -1)
    blocks = v.reshape(v.shape[:-1] + (-1, 32))
    amax = np.abs(blocks).max(-1, keepdims=True)
    byte = np.maximum(np.where(amax > 0, np.frexp(amax)[1] - 1 + 127, 0) - down, 1)
    scale = np.exp2(byte - 127.0)
    codes = (blocks / scale).astype(np.float32).astype(dtype).astype(np.float64)
    return np.moveaxis((codes * scale).reshape(v.shape), -1, axis)


WIDE = False


def mx_kscale(k):
    if not WIDE:
        return np.ones(k)
    levels = np.array([20, -20, 10, -10, 0])
    a = np.random.permutation(np.resize(levels, k // 512 * 4)).reshape(k // 512, 4)
    idx = np.arange(k)
    return np.exp2(a[idx // 512, idx % 128 // 32])


BF16 = ml_dtypes.bfloat16


def bf(x):
    return np.asarray(x, np.float32).astype(BF16)


def f64(x):
    return np.asarray(x).astype(np.float64)


BATCH, IN_Q, OUT_Q = 4096, 256, 128
K, N = 4 * IN_Q, 4 * OUT_Q


def _quat_block_matrix(W):
    Ww, Wx, Wy, Wz = W[..., 0], W[..., 1], W[..., 2], W[..., 3]
    row_w = np.stack([Ww, -Wx, -Wy, -Wz], axis=0)
    row_x = np.stack([Wx, Ww, -Wz, Wy], axis=0)
    row_y = np.stack([Wy, Wz, Ww, -Wx], axis=0)
    row_z = np.stack([Wz, -Wy, Wx, Ww], axis=0)
    return np.stack([row_w, row_x, row_y, row_z], axis=0)


def _mk(W):
    return _quat_block_matrix(W).transpose(3, 1, 2, 0).reshape(K, N)


def setup_inputs():
    u = mx_kscale(N)[::4]
    sigma = 1.0 / np.sqrt(2.0 * (IN_Q + OUT_Q))
    x = bf(np.random.standard_normal((BATCH, IN_Q, 4)))
    W0 = bf(np.random.standard_normal((OUT_Q, IN_Q, 4)) * sigma)
    B = bf(np.random.standard_normal((OUT_Q, 4)) * 0.2)
    g = bf(np.random.standard_normal((BATCH, OUT_Q, 4)) * np.exp2(np.random.randint(-12, 1, (BATCH, 1, 1))) * 32.0 * u[None, :, None])
    z = (f64(x).reshape(BATCH, K) @ _mk(f64(W0))).reshape(BATCH, OUT_Q, 4) + f64(B)
    return {"x": x, "W": bf(f64(W0) / u[:, None, None]), "B": B, "z": np.asarray(z, np.float32), "grad_out": g}


def reference(x, W, B, z, grad_out):
    t = np.tanh(f64(z))
    dz = (f64(grad_out) * (1.0 - t * t)).reshape(BATCH, N)
    Wt = f64(W).transpose(1, 0, 2).reshape(IN_Q, N)
    Wq = mxq(Wt, 1, "e4m3").reshape(IN_Q, OUT_Q, 4).transpose(1, 0, 2)
    Mk = _mk(Wq)
    return (mxq(dz, 1, "e5m2") @ Mk.T).reshape(BATCH, IN_Q, 4)

@@ -1,0 +1,179 @@
+from contextlib import ExitStack
+
+import concourse.mybir as mybir
+from concourse.masks import make_identity
+
+F32 = mybir.dt.float32
+BF16 = mybir.dt.bfloat16
+U32 = mybir.dt.uint32
+U8 = mybir.dt.uint8
+E4M3_X4 = mybir.dt.float8_e4m3fn_x4
+E5M2_X4 = mybir.dt.float8_e5m2_x4
+ACT = mybir.ActivationFunctionType
+ALU = mybir.AluOpType
+
+BATCH, IN_Q, OUT_Q = 4096, 256, 128
+P = 128
+COMP = 4
+K = COMP * OUT_Q
+N_OUT = COMP * IN_Q
+BANK = 512
+HALVES = N_OUT // BANK
+I_HALF = IN_Q // HALVES
+TILES = BATCH // P
+PAIR = 2
+STEPS = TILES // PAIR
+LOAD_MAX = 8
+
+FLOPS = 2 * BATCH * K * N_OUT
+BYTES = 4 * BATCH * K + 2 * BATCH * K + 2 * OUT_Q * IN_Q * COMP + 4 * BATCH * N_OUT
+
+SIGN = (
+    (1.0, 1.0, 1.0, 1.0),
+    (-1.0, 1.0, 1.0, -1.0),
+    (-1.0, -1.0, 1.0, 1.0),
+    (-1.0, 1.0, -1.0, 1.0),
+)
+
+
+def tile_quatnetpytorchdenselayer_t_v_kernel(tc, x, W, B, z, grad_out, out):
+    nc = tc.nc
+
+    z_rows = z.rearrange("(p j) o d -> p j (o d)", j=TILES)
+    g_rows = grad_out.rearrange("(p j) o d -> p j (o d)", j=TILES)
+    out_rows = out.rearrange("(p j) i c -> p j (i c)", j=TILES)
+
+    with ExitStack() as stack:
+        stack.enter_context(tc.manual_schedule())
+        keep = stack.enter_context(tc.tile_pool(name="keep", bufs=1))
+        work = stack.enter_context(tc.tile_pool(name="work", bufs=2))
+        psum = stack.enter_context(tc.psum_pool(name="psum", bufs=2))
+
+        w_sb = keep.tile([P, HALVES, I_HALF, COMP], BF16)
+        nc.sync.dma_start(out=w_sb[:], in_=W.rearrange("o (h i) e -> o h i e", h=HALVES))
+        z_all = keep.tile([P, TILES, K], F32)
+        g_all = keep.tile([P, TILES, K], BF16)
+        first, count = 0, PAIR
+        while first < TILES:
+            tiles = slice(first, first + count)
+            nc.sync.dma_start(out=z_all[:, tiles, :], in_=z_rows[:, tiles, :])
+            nc.sync.dma_start(out=g_all[:, tiles, :], in_=g_rows[:, tiles, :])
+            first += count
+            count = min(first, LOAD_MAX)
+
+        identity = keep.tile([P, P], F32)
+        make_identity(nc, identity[:])
+
+        mk_bf = keep.tile([P, HALVES, COMP, I_HALF, COMP], BF16, align_bytes=64)
+        for c in range(COMP):
+            for d in range(COMP):
+                nc.vector.tensor_scalar_mul(
+                    out=mk_bf[:, :, c, :, d], in0=w_sb[:, :, :, c ^ d], scalar1=-SIGN[c][d]
+                )
+        mk_codes = keep.tile([P, N_OUT], U32, align_bytes=64)
+        mk_scales = keep.tile([P, N_OUT], U8, align_bytes=64)
+        nc.vector.quantize_mx(
+            out=mk_codes[:].bitcast(E4M3_X4),
+            scales=mk_scales[:],
+            in_=mk_bf[:].rearrange("o h c i d -> o (h c i d)"),
+        )
+
+        tanhs, squares, turneds, groupeds, operands, products, results = {}, {}, {}, {}, {}, {}, {}
+
+        def tanh(k):
+            t = work.tile([P, PAIR * K], F32)
+            nc.scalar.activation(
+                out=t[:],
+                in_=z_all[:, PAIR * k : PAIR * (k + 1), :].rearrange("p j n -> p (j n)"),
+                func=ACT.Tanh,
+            )
+            tanhs[k] = t
+
+        def square(k):
+            t2 = work.tile([P, PAIR * K], F32, bufs=3)
+            nc.scalar.activation(out=t2[:], in_=tanhs[k][:], func=ACT.Square)
+            squares[k] = t2
+
+        def gradient_and_turn(k):
+            minus_dz = work.tile([P, PAIR * K], BF16)
+            nc.vector.scalar_tensor_tensor(
+                out=minus_dz[:],
+                in0=squares[k][:],
+                scalar=1.0,
+                in1=g_all[:, PAIR * k : PAIR * (k + 1), :].rearrange("p j n -> p (j n)"),
+                op0=ALU.subtract,
+                op1=ALU.mult,
+            )
+            words = minus_dz[:].bitcast(F32).rearrange("p (j o u) -> p j u o", j=PAIR, u=2)
+            turned = psum.tile([P, 2, PAIR * P], F32)
+            for j in range(PAIR):
+                for u in range(2):
+                    nc.tensor.transpose(
+                        out=turned[:, u, j * P : (j + 1) * P], in_=words[:, j, u, :], identity=identity[:]
+                    )
+            turneds[k] = turned
+
+        def regroup(k):
+            grouped = work.tile([P, PAIR * P * COMP], BF16, align_bytes=64)
+            nc.vector.tensor_copy(
+                out=grouped[:].bitcast(F32).rearrange("o (b u) -> o b u", u=2),
+                in_=turneds[k][:].rearrange("o u b -> o b u"),
+            )
+            groupeds[k] = grouped
+
+        def quantise(k):
+            dz_codes = work.tile([P, PAIR * P], U32, bufs=3, align_bytes=64)
+            dz_scales = work.tile([P, PAIR * P], U8, bufs=3, align_bytes=64)
+            nc.vector.quantize_mx(out=dz_codes[:].bitcast(E5M2_X4), scales=dz_scales[:], in_=groupeds[k][:])
+            operands[k] = (dz_codes, dz_scales)
+
+        def multiply(k):
+            dz_codes, dz_scales = operands[k]
+            for j in range(PAIR):
+                rows = slice(j * P, (j + 1) * P)
+                for h in range(HALVES):
+                    cols = slice(h * BANK, (h + 1) * BANK)
+                    product = psum.tile([P, BANK], F32, bufs=6)
+                    nc.tensor.matmul_mx(
+                        out=product[:],
+                        lhsT=dz_codes[:, rows].bitcast(E5M2_X4),
+                        lhsT_scale=dz_scales[:, rows],
+                        rhs=mk_codes[:, cols].bitcast(E4M3_X4),
+                        rhs_scale=mk_scales[:, cols],
+                        start=True,
+                        stop=True,
+                    )
+                    products[(k, j, h)] = product
+            result = work.tile([P, PAIR, N_OUT], F32, bufs=8)
+            results[k] = result
+
+        def leave_psum(k, j):
+            for h in range(HALVES):
+                dest = results[k][:, j, h * BANK : (h + 1) * BANK].rearrange("p (i c) -> p i c", c=COMP)
+                source = products[(k, j, h)][:].rearrange("p (c i) -> p i c", c=COMP)
+                if h == 0:
+                    nc.vector.tensor_copy(out=dest, in_=source)
+                else:
+                    nc.scalar.copy(out=dest, in_=source)
+
+        def store(k):
+            nc.sync.dma_start(out=out_rows[:, PAIR * k : PAIR * (k + 1), :], in_=results[k][:])
+
+        for r in range(STEPS + 3):
+            if 0 <= r - 3:
+                multiply(r - 3)
+            if 0 <= r - 2 < STEPS:
+                regroup(r - 2)
+            if r < STEPS:
+                tanh(r)
+            if 0 <= r - 1 < STEPS:
+                gradient_and_turn(r - 1)
+            if 0 <= r - 2 < STEPS:
+                quantise(r - 2)
+            if 0 <= r - 3:
+                leave_psum(r - 3, 0)
+            if r < STEPS:
+                square(r)
+            if 0 <= r - 3:
+                leave_psum(r - 3, 1)
+                store(r - 3)

@@ -49,8 +49,8 @@ def tile_quatnetpytorchdenselayer_t_v_kernel(tc, x, W, B, z, grad_out, out):
         work = stack.enter_context(tc.tile_pool(name="work", bufs=2))
         psum = stack.enter_context(tc.psum_pool(name="psum", bufs=2))
 
-        w_sb = keep.tile([P, HALVES, I_HALF, COMP], BF16)
-        nc.sync.dma_start(out=w_sb[:], in_=W.rearrange("o (h i) e -> o h i e", h=HALVES))
+        mk_bf = keep.tile([P, HALVES, COMP, I_HALF, COMP], BF16, align_bytes=64)
+        nc.sync.dma_start(out=mk_bf[:, :, 0, :, :], in_=W.rearrange("o (h i) e -> o h i e", h=HALVES))
         z_all = keep.tile([P, TILES, K], F32)
         g_all = keep.tile([P, TILES, K], BF16)
         first, count = 0, PAIR
@@ -64,11 +64,23 @@ def tile_quatnetpytorchdenselayer_t_v_kernel(tc, x, W, B, z, grad_out, out):
         identity = keep.tile([P, P], F32)
         make_identity(nc, identity[:])
 
-        mk_bf = keep.tile([P, HALVES, COMP, I_HALF, COMP], BF16, align_bytes=64)
+        signs = keep.tile([P, COMP, COMP], BF16)
+        nc.vector.memset(signs[:], 1.0)
         for c in range(COMP):
             for d in range(COMP):
-                nc.vector.tensor_scalar_mul(
-                    out=mk_bf[:, :, c, :, d], in0=w_sb[:, :, :, c ^ d], scalar1=-SIGN[c][d]
+                if SIGN[c][d] < 0:
+                    nc.vector.memset(signs[:, c, d : d + 1], -1.0)
+        for h in range(HALVES):
+            w_pairs = mk_bf[:, h, 0, :, :].rearrange("o i (a b) -> o i a b", b=2)
+            for c in range(1, COMP):
+                nc.vector.tensor_tensor(
+                    out=mk_bf[:, h, c, :, :].rearrange("o i (a b) -> o i a b", b=2),
+                    in0=w_pairs[:, :, :: (-1 if c & 2 else 1), :: (-1 if c & 1 else 1)],
+                    in1=signs[:, c, :]
+                    .rearrange("o (a b) -> o a b", b=2)
+                    .unsqueeze(1)
+                    .to_broadcast([P, I_HALF, 2, 2]),
+                    op=ALU.mult,
                 )
         mk_codes = keep.tile([P, N_OUT], U32, align_bytes=64)
         mk_scales = keep.tile([P, N_OUT], U8, align_bytes=64)
@@ -152,9 +164,9 @@ def tile_quatnetpytorchdenselayer_t_v_kernel(tc, x, W, B, z, grad_out, out):
                 dest = results[k][:, j, h * BANK : (h + 1) * BANK].rearrange("p (i c) -> p i c", c=COMP)
                 source = products[(k, j, h)][:].rearrange("p (c i) -> p i c", c=COMP)
                 if h == 0:
-                    nc.vector.tensor_copy(out=dest, in_=source)
+                    nc.vector.tensor_scalar_mul(out=dest, in0=source, scalar1=-1.0)
                 else:
-                    nc.scalar.copy(out=dest, in_=source)
+                    nc.scalar.mul(out=dest, in_=source, mul=-1.0)
 
         def store(k):
             nc.sync.dma_start(out=out_rows[:, PAIR * k : PAIR * (k + 1), :], in_=results[k][:])

@@ -143,7 +143,7 @@ def tile_quatnetpytorchdenselayer_t_v_kernel(tc, x, W, B, z, grad_out, out):
             dz_codes, dz_scales = operands[k]
             for j in range(PAIR):
                 rows = slice(j * P, (j + 1) * P)
-                for h in range(HALVES):
+                for h in reversed(range(HALVES)):
                     cols = slice(h * BANK, (h + 1) * BANK)
                     product = psum.tile([P, BANK], F32, bufs=6)
                     nc.tensor.matmul_mx(
@@ -174,18 +174,18 @@ def tile_quatnetpytorchdenselayer_t_v_kernel(tc, x, W, B, z, grad_out, out):
         for r in range(STEPS + 3):
             if 0 <= r - 3:
                 multiply(r - 3)
-            if 0 <= r - 2 < STEPS:
-                regroup(r - 2)
             if r < STEPS:
                 tanh(r)
             if 0 <= r - 1 < STEPS:
                 gradient_and_turn(r - 1)
             if 0 <= r - 2 < STEPS:
-                quantise(r - 2)
+                regroup(r - 2)
             if 0 <= r - 3:
                 leave_psum(r - 3, 0)
             if r < STEPS:
                 square(r)
+            if 0 <= r - 2 < STEPS:
+                quantise(r - 2)
             if 0 <= r - 3:
                 leave_psum(r - 3, 1)
                 store(r - 3)

@@ -160,16 +160,20 @@ def tile_quatnetpytorchdenselayer_t_v_kernel(tc, x, W, B, z, grad_out, out):
             results[k] = result
 
         def leave_psum(k, j):
-            for h in range(HALVES):
+            vector_helps = k < STEPS - 3 or k == STEPS - 1 or (k == STEPS - 2 and j == PAIR - 1)
+            for h in reversed(range(HALVES)):
                 dest = results[k][:, j, h * BANK : (h + 1) * BANK].rearrange("p (i c) -> p i c", c=COMP)
                 source = products[(k, j, h)][:].rearrange("p (c i) -> p i c", c=COMP)
-                if h == 0:
+                if h == 0 and vector_helps:
                     nc.vector.tensor_scalar_mul(out=dest, in0=source, scalar1=-1.0)
                 else:
                     nc.scalar.mul(out=dest, in_=source, mul=-1.0)
 
-        def store(k):
-            nc.sync.dma_start(out=out_rows[:, PAIR * k : PAIR * (k + 1), :], in_=results[k][:])
+        def store(k, first, count):
+            nc.sync.dma_start(
+                out=out_rows[:, PAIR * k + first : PAIR * k + first + count, :],
+                in_=results[k][:, first : first + count, :],
+            )
 
         for r in range(STEPS + 3):
             if 0 <= r - 3:
@@ -182,10 +186,15 @@ def tile_quatnetpytorchdenselayer_t_v_kernel(tc, x, W, B, z, grad_out, out):
                 regroup(r - 2)
             if 0 <= r - 3:
                 leave_psum(r - 3, 0)
+            if r - 3 == STEPS - 1:
+                store(r - 3, 0, 1)
             if r < STEPS:
                 square(r)
             if 0 <= r - 2 < STEPS:
                 quantise(r - 2)
             if 0 <= r - 3:
                 leave_psum(r - 3, 1)
-                store(r - 3)
+                if r - 3 == STEPS - 1:
+                    store(r - 3, 1, 1)
+                else:
+                    store(r - 3, 0, PAIR)

@@ -23,7 +23,10 @@ I_HALF = IN_Q // HALVES
 TILES = BATCH // P
 PAIR = 2
 STEPS = TILES // PAIR
-LOAD_MAX = 8
+LOAD_MAX = 16
+STORE_GROUPS = (4, 3, 2, 1, 1, 1, 1, 1, 1, 1)
+RING = 10
+assert sum(STORE_GROUPS) == STEPS
 
 FLOPS = 2 * BATCH * K * N_OUT
 BYTES = 4 * BATCH * K + 2 * BATCH * K + 2 * OUT_Q * IN_Q * COMP + 4 * BATCH * N_OUT
@@ -90,7 +93,14 @@ def tile_quatnetpytorchdenselayer_t_v_kernel(tc, x, W, B, z, grad_out, out):
             in_=mk_bf[:].rearrange("o h c i d -> o (h c i d)"),
         )
 
-        tanhs, squares, turneds, groupeds, operands, products, results = {}, {}, {}, {}, {}, {}, {}
+        tanhs, squares, turneds, groupeds, operands, products = {}, {}, {}, {}, {}, {}
+        ring = keep.tile([P, RING * PAIR, N_OUT], F32)
+        group_first = {}
+        first_step = 0
+        for size in STORE_GROUPS:
+            assert first_step % RING + size <= RING
+            group_first[first_step + size - 1] = first_step
+            first_step += size
 
         def tanh(k):
             t = work.tile([P, PAIR * K], F32)
@@ -156,23 +166,24 @@ def tile_quatnetpytorchdenselayer_t_v_kernel(tc, x, W, B, z, grad_out, out):
                         stop=True,
                     )
                     products[(k, j, h)] = product
-            result = work.tile([P, PAIR, N_OUT], F32, bufs=8)
-            results[k] = result
 
         def leave_psum(k, j):
             vector_helps = k < STEPS - 3 or k == STEPS - 1 or (k == STEPS - 2 and j == PAIR - 1)
             for h in reversed(range(HALVES)):
-                dest = results[k][:, j, h * BANK : (h + 1) * BANK].rearrange("p (i c) -> p i c", c=COMP)
+                dest = ring[:, PAIR * (k % RING) + j, h * BANK : (h + 1) * BANK].rearrange(
+                    "p (i c) -> p i c", c=COMP
+                )
                 source = products[(k, j, h)][:].rearrange("p (c i) -> p i c", c=COMP)
                 if h == 0 and vector_helps:
                     nc.vector.tensor_scalar_mul(out=dest, in0=source, scalar1=-1.0)
                 else:
                     nc.scalar.mul(out=dest, in_=source, mul=-1.0)
 
-        def store(k, first, count):
+        def store(first, last):
+            place = PAIR * (first % RING)
             nc.sync.dma_start(
-                out=out_rows[:, PAIR * k + first : PAIR * k + first + count, :],
-                in_=results[k][:, first : first + count, :],
+                out=out_rows[:, PAIR * first : PAIR * (last + 1), :],
+                in_=ring[:, place : place + PAIR * (last + 1 - first), :],
             )
 
         for r in range(STEPS + 3):
@@ -186,15 +197,11 @@ def tile_quatnetpytorchdenselayer_t_v_kernel(tc, x, W, B, z, grad_out, out):
                 regroup(r - 2)
             if 0 <= r - 3:
                 leave_psum(r - 3, 0)
-            if r - 3 == STEPS - 1:
-                store(r - 3, 0, 1)
             if r < STEPS:
                 square(r)
             if 0 <= r - 2 < STEPS:
                 quantise(r - 2)
             if 0 <= r - 3:
                 leave_psum(r - 3, 1)
-                if r - 3 == STEPS - 1:
-                    store(r - 3, 1, 1)
-                else:
-                    store(r - 3, 0, PAIR)
+                if r - 3 in group_first:
+                    store(group_first[r - 3], r - 3)

@@ -169,12 +169,13 @@ def tile_quatnetpytorchdenselayer_t_v_kernel(tc, x, W, B, z, grad_out, out):
 
         def leave_psum(k, j):
             vector_helps = k < STEPS - 3 or k == STEPS - 1 or (k == STEPS - 2 and j == PAIR - 1)
+            vector_alone = k < STEPS - 3 and k % 4 == 3 and j == PAIR - 1
             for h in reversed(range(HALVES)):
                 dest = ring[:, PAIR * (k % RING) + j, h * BANK : (h + 1) * BANK].rearrange(
                     "p (i c) -> p i c", c=COMP
                 )
                 source = products[(k, j, h)][:].rearrange("p (c i) -> p i c", c=COMP)
-                if h == 0 and vector_helps:
+                if (h == 0 and vector_helps) or vector_alone:
                     nc.vector.tensor_scalar_mul(out=dest, in0=source, scalar1=-1.0)
                 else:
                     nc.scalar.mul(out=dest, in_=source, mul=-1.0)

@@ -23,6 +23,7 @@ I_HALF = IN_Q // HALVES
 TILES = BATCH // P
 PAIR = 2
 STEPS = TILES // PAIR
+GP_COLS = 256
 LOAD_MAX = 16
 STORE_GROUPS = (4, 3, 2, 1, 1, 1, 1, 1, 1, 1)
 RING = 10
@@ -53,13 +54,16 @@ def tile_quatnetpytorchdenselayer_t_v_kernel(tc, x, W, B, z, grad_out, out):
         psum = stack.enter_context(tc.psum_pool(name="psum", bufs=2))
 
         mk_bf = keep.tile([P, HALVES, COMP, I_HALF, COMP], BF16, align_bytes=64)
-        nc.sync.dma_start(out=mk_bf[:, :, 0, :, :], in_=W.rearrange("o (h i) e -> o h i e", h=HALVES))
         z_all = keep.tile([P, TILES, K], F32)
         g_all = keep.tile([P, TILES, K], BF16)
         first, count = 0, PAIR
         while first < TILES:
             tiles = slice(first, first + count)
             nc.sync.dma_start(out=z_all[:, tiles, :], in_=z_rows[:, tiles, :])
+            if first == 0:
+                nc.sync.dma_start(
+                    out=mk_bf[:, :, 0, :, :], in_=W.rearrange("o (h i) e -> o h i e", h=HALVES)
+                )
             nc.sync.dma_start(out=g_all[:, tiles, :], in_=g_rows[:, tiles, :])
             first += count
             count = min(first, LOAD_MAX)
@@ -87,11 +91,13 @@ def tile_quatnetpytorchdenselayer_t_v_kernel(tc, x, W, B, z, grad_out, out):
                 )
         mk_codes = keep.tile([P, N_OUT], U32, align_bytes=64)
         mk_scales = keep.tile([P, N_OUT], U8, align_bytes=64)
-        nc.vector.quantize_mx(
-            out=mk_codes[:].bitcast(E4M3_X4),
-            scales=mk_scales[:],
-            in_=mk_bf[:].rearrange("o h c i d -> o (h c i d)"),
-        )
+
+        def quantise_mk():
+            nc.vector.quantize_mx(
+                out=mk_codes[:].bitcast(E4M3_X4),
+                scales=mk_scales[:],
+                in_=mk_bf[:].rearrange("o h c i d -> o (h c i d)"),
+            )
 
         tanhs, squares, turneds, groupeds, operands, products = {}, {}, {}, {}, {}, {}
         ring = keep.tile([P, RING * PAIR, N_OUT], F32)
@@ -111,16 +117,37 @@ def tile_quatnetpytorchdenselayer_t_v_kernel(tc, x, W, B, z, grad_out, out):
             )
             tanhs[k] = t
 
+        def gp_helps(k):
+            return 3 <= k < STEPS
+
+        own = PAIR * K - GP_COLS
+        square_tile = keep.tile([P, own + GP_COLS + own], F32)
+
+        def square_run(k):
+            return square_tile[:, : PAIR * K] if k % 2 == 0 else square_tile[:, own:]
+
+        def gp_columns(k):
+            return slice(own, PAIR * K) if k % 2 == 0 else slice(0, GP_COLS)
+
         def square(k):
-            t2 = work.tile([P, PAIR * K], F32, bufs=3)
-            nc.scalar.activation(out=t2[:], in_=tanhs[k][:], func=ACT.Square)
-            squares[k] = t2
+            mine = slice(0, PAIR * K)
+            if gp_helps(k):
+                mine = slice(0, own) if k % 2 == 0 else slice(GP_COLS, PAIR * K)
+                squares[k] = square_run(k)
+            else:
+                t2 = work.tile([P, PAIR * K], F32, bufs=3)
+                squares[k] = t2[:]
+            nc.scalar.activation(out=squares[k][:, mine], in_=tanhs[k][:, mine], func=ACT.Square)
+
+        def gp_square(k):
+            t = tanhs[k][:, gp_columns(k)]
+            nc.gpsimd.tensor_tensor(out=square_run(k)[:, gp_columns(k)], in0=t, in1=t, op=ALU.mult)
 
         def gradient_and_turn(k):
             minus_dz = work.tile([P, PAIR * K], BF16)
             nc.vector.scalar_tensor_tensor(
                 out=minus_dz[:],
-                in0=squares[k][:],
+                in0=squares[k],
                 scalar=1.0,
                 in1=g_all[:, PAIR * k : PAIR * (k + 1), :].rearrange("p j n -> p (j n)"),
                 op0=ALU.subtract,
@@ -169,7 +196,7 @@ def tile_quatnetpytorchdenselayer_t_v_kernel(tc, x, W, B, z, grad_out, out):
 
         def leave_psum(k, j):
             vector_helps = k < STEPS - 3 or k == STEPS - 1 or (k == STEPS - 2 and j == PAIR - 1)
-            vector_alone = k < STEPS - 3 and k % 4 == 3 and j == PAIR - 1
+            vector_alone = False
             for h in reversed(range(HALVES)):
                 dest = ring[:, PAIR * (k % RING) + j, h * BANK : (h + 1) * BANK].rearrange(
                     "p (i c) -> p i c", c=COMP
@@ -194,15 +221,20 @@ def tile_quatnetpytorchdenselayer_t_v_kernel(tc, x, W, B, z, grad_out, out):
                 tanh(r)
             if 0 <= r - 1 < STEPS:
                 gradient_and_turn(r - 1)
+            if r == 1:
+                quantise_mk()
             if 0 <= r - 2 < STEPS:
                 regroup(r - 2)
             if 0 <= r - 3:
                 leave_psum(r - 3, 0)
+            if r < STEPS and gp_helps(r):
+                gp_square(r)
             if r < STEPS:
                 square(r)
+            if 0 <= r - 3:
+                leave_psum(r - 3, 1)
             if 0 <= r - 2 < STEPS:
                 quantise(r - 2)
             if 0 <= r - 3:
-                leave_psum(r - 3, 1)
                 if r - 3 in group_first:
                     store(group_first[r - 3], r - 3)

@@ -25,8 +25,7 @@ PAIR = 2
 STEPS = TILES // PAIR
 GP_COLS = 256
 LOAD_MAX = 16
-STORE_GROUPS = (4, 3, 2, 1, 1, 1, 1, 1, 1, 1)
-RING = 10
+STORE_GROUPS = (5, 3, 2, 2, 2, 2)
 assert sum(STORE_GROUPS) == STEPS
 
 FLOPS = 2 * BATCH * K * N_OUT
@@ -53,8 +52,14 @@ def tile_quatnetpytorchdenselayer_t_v_kernel(tc, x, W, B, z, grad_out, out):
         work = stack.enter_context(tc.tile_pool(name="work", bufs=2))
         psum = stack.enter_context(tc.psum_pool(name="psum", bufs=2))
 
-        mk_bf = keep.tile([P, HALVES, COMP, I_HALF, COMP], BF16, align_bytes=64)
-        z_all = keep.tile([P, TILES, K], F32)
+        mk_bf = keep.tile([P, HALVES * COMP, I_HALF, COMP], BF16, align_bytes=64)
+
+        def place(h, c):
+            return COMP - 1 - c if h == 0 else COMP + c
+
+        shared = keep.tile([P, TILES * N_OUT], F32)
+        results = shared[:].rearrange("p (j n) -> p j n", n=N_OUT)
+        z_all = shared[:, TILES * (N_OUT - K) :].rearrange("p (j n) -> p j n", n=K)
         g_all = keep.tile([P, TILES, K], BF16)
         first, count = 0, PAIR
         while first < TILES:
@@ -62,9 +67,11 @@ def tile_quatnetpytorchdenselayer_t_v_kernel(tc, x, W, B, z, grad_out, out):
             nc.sync.dma_start(out=z_all[:, tiles, :], in_=z_rows[:, tiles, :])
             if first == 0:
                 nc.sync.dma_start(
-                    out=mk_bf[:, :, 0, :, :], in_=W.rearrange("o (h i) e -> o h i e", h=HALVES)
+                    out=mk_bf[:, COMP - 1 : COMP + 1, :, :], in_=W.rearrange("o (h i) e -> o h i e", h=HALVES)
                 )
-            nc.sync.dma_start(out=g_all[:, tiles, :], in_=g_rows[:, tiles, :])
+            if first > 0:
+                g_tiles = slice(0 if first == PAIR else first, first + count)
+                nc.sync.dma_start(out=g_all[:, g_tiles, :], in_=g_rows[:, g_tiles, :])
             first += count
             count = min(first, LOAD_MAX)
 
@@ -78,10 +85,10 @@ def tile_quatnetpytorchdenselayer_t_v_kernel(tc, x, W, B, z, grad_out, out):
                 if SIGN[c][d] < 0:
                     nc.vector.memset(signs[:, c, d : d + 1], -1.0)
         for h in range(HALVES):
-            w_pairs = mk_bf[:, h, 0, :, :].rearrange("o i (a b) -> o i a b", b=2)
+            w_pairs = mk_bf[:, place(h, 0), :, :].rearrange("o i (a b) -> o i a b", b=2)
             for c in range(1, COMP):
                 nc.vector.tensor_tensor(
-                    out=mk_bf[:, h, c, :, :].rearrange("o i (a b) -> o i a b", b=2),
+                    out=mk_bf[:, place(h, c), :, :].rearrange("o i (a b) -> o i a b", b=2),
                     in0=w_pairs[:, :, :: (-1 if c & 2 else 1), :: (-1 if c & 1 else 1)],
                     in1=signs[:, c, :]
                     .rearrange("o (a b) -> o a b", b=2)
@@ -96,15 +103,13 @@ def tile_quatnetpytorchdenselayer_t_v_kernel(tc, x, W, B, z, grad_out, out):
             nc.vector.quantize_mx(
                 out=mk_codes[:].bitcast(E4M3_X4),
                 scales=mk_scales[:],
-                in_=mk_bf[:].rearrange("o h c i d -> o (h c i d)"),
+                in_=mk_bf[:].rearrange("o m i d -> o (m i d)"),
             )
 
         tanhs, squares, turneds, groupeds, operands, products = {}, {}, {}, {}, {}, {}
-        ring = keep.tile([P, RING * PAIR, N_OUT], F32)
         group_first = {}
         first_step = 0
         for size in STORE_GROUPS:
-            assert first_step % RING + size <= RING
             group_first[first_step + size - 1] = first_step
             first_step += size
 
@@ -198,21 +203,20 @@ def tile_quatnetpytorchdenselayer_t_v_kernel(tc, x, W, B, z, grad_out, out):
             vector_helps = k < STEPS - 3 or k == STEPS - 1 or (k == STEPS - 2 and j == PAIR - 1)
             vector_alone = False
             for h in reversed(range(HALVES)):
-                dest = ring[:, PAIR * (k % RING) + j, h * BANK : (h + 1) * BANK].rearrange(
+                dest = results[:, PAIR * k + j, h * BANK : (h + 1) * BANK].rearrange(
                     "p (i c) -> p i c", c=COMP
                 )
                 source = products[(k, j, h)][:].rearrange("p (c i) -> p i c", c=COMP)
+                if h == 0:
+                    source = source[:, :, ::-1]
                 if (h == 0 and vector_helps) or vector_alone:
                     nc.vector.tensor_scalar_mul(out=dest, in0=source, scalar1=-1.0)
                 else:
                     nc.scalar.mul(out=dest, in_=source, mul=-1.0)
 
         def store(first, last):
-            place = PAIR * (first % RING)
-            nc.sync.dma_start(
-                out=out_rows[:, PAIR * first : PAIR * (last + 1), :],
-                in_=ring[:, place : place + PAIR * (last + 1 - first), :],
-            )
+            tiles = slice(PAIR * first, PAIR * (last + 1))
+            nc.sync.dma_start(out=out_rows[:, tiles, :], in_=results[:, tiles, :])
 
         for r in range(STEPS + 3):
             if 0 <= r - 3:

@@ -235,10 +235,9 @@ def tile_quatnetpytorchdenselayer_t_v_kernel(tc, x, W, B, z, grad_out, out):
                 gp_square(r)
             if r < STEPS:
                 square(r)
-            if 0 <= r - 3:
-                leave_psum(r - 3, 1)
             if 0 <= r - 2 < STEPS:
                 quantise(r - 2)
             if 0 <= r - 3:
+                leave_psum(r - 3, 1)
                 if r - 3 in group_first:
                     store(group_first[r - 3], r - 3)

@@ -52,15 +52,15 @@ def tile_quatnetpytorchdenselayer_t_v_kernel(tc, x, W, B, z, grad_out, out):
         work = stack.enter_context(tc.tile_pool(name="work", bufs=2))
         psum = stack.enter_context(tc.psum_pool(name="psum", bufs=2))
 
-        mk_bf = keep.tile([P, HALVES * COMP, I_HALF, COMP], BF16, align_bytes=64)
+        mk_bf = keep.tile([P, HALVES * COMP, I_HALF, COMP], BF16, align_bytes=512)
 
         def place(h, c):
             return COMP - 1 - c if h == 0 else COMP + c
 
-        shared = keep.tile([P, TILES * N_OUT], F32)
+        shared = keep.tile([P, TILES * N_OUT], F32, align_bytes=512)
         results = shared[:].rearrange("p (j n) -> p j n", n=N_OUT)
         z_all = shared[:, TILES * (N_OUT - K) :].rearrange("p (j n) -> p j n", n=K)
-        g_all = keep.tile([P, TILES, K], BF16)
+        g_all = keep.tile([P, TILES, K], BF16, align_bytes=512)
         first, count = 0, PAIR
         while first < TILES:
             tiles = slice(first, first + count)

@@ -52,15 +52,15 @@ def tile_quatnetpytorchdenselayer_t_v_kernel(tc, x, W, B, z, grad_out, out):
         work = stack.enter_context(tc.tile_pool(name="work", bufs=2))
         psum = stack.enter_context(tc.psum_pool(name="psum", bufs=2))
 
-        mk_bf = keep.tile([P, HALVES * COMP, I_HALF, COMP], BF16, align_bytes=512)
+        mk_bf = keep.tile([P, HALVES * COMP, I_HALF, COMP], BF16, align_bytes=4096)
 
         def place(h, c):
             return COMP - 1 - c if h == 0 else COMP + c
 
-        shared = keep.tile([P, TILES * N_OUT], F32, align_bytes=512)
+        shared = keep.tile([P, TILES * N_OUT], F32, align_bytes=4096)
         results = shared[:].rearrange("p (j n) -> p j n", n=N_OUT)
         z_all = shared[:, TILES * (N_OUT - K) :].rearrange("p (j n) -> p j n", n=K)
-        g_all = keep.tile([P, TILES, K], BF16, align_bytes=512)
+        g_all = keep.tile([P, TILES, K], BF16, align_bytes=4096)
         first, count = 0, PAIR
         while first < TILES:
             tiles = slice(first, first + count)

from contextlib import ExitStack

import concourse.mybir as mybir
from concourse.masks import make_identity

F32 = mybir.dt.float32
BF16 = mybir.dt.bfloat16
U32 = mybir.dt.uint32
U8 = mybir.dt.uint8
E4M3_X4 = mybir.dt.float8_e4m3fn_x4
E5M2_X4 = mybir.dt.float8_e5m2_x4
ACT = mybir.ActivationFunctionType
ALU = mybir.AluOpType

BATCH, IN_Q, OUT_Q = 4096, 256, 128
P = 128
COMP = 4
K = COMP * OUT_Q
N_OUT = COMP * IN_Q
BANK = 512
HALVES = N_OUT // BANK
I_HALF = IN_Q // HALVES
TILES = BATCH // P
PAIR = 2
STEPS = TILES // PAIR
GP_COLS = 256
LOAD_MAX = 16
STORE_GROUPS = (5, 3, 2, 2, 2, 2)
assert sum(STORE_GROUPS) == STEPS

FLOPS = 2 * BATCH * K * N_OUT
BYTES = 4 * BATCH * K + 2 * BATCH * K + 2 * OUT_Q * IN_Q * COMP + 4 * BATCH * N_OUT

SIGN = (
    (1.0, 1.0, 1.0, 1.0),
    (-1.0, 1.0, 1.0, -1.0),
    (-1.0, -1.0, 1.0, 1.0),
    (-1.0, 1.0, -1.0, 1.0),
)


def tile_quatnetpytorchdenselayer_t_v_kernel(tc, x, W, B, z, grad_out, out):
    nc = tc.nc

    z_rows = z.rearrange("(p j) o d -> p j (o d)", j=TILES)
    g_rows = grad_out.rearrange("(p j) o d -> p j (o d)", j=TILES)
    out_rows = out.rearrange("(p j) i c -> p j (i c)", j=TILES)

    with ExitStack() as stack:
        stack.enter_context(tc.manual_schedule())
        keep = stack.enter_context(tc.tile_pool(name="keep", bufs=1))
        work = stack.enter_context(tc.tile_pool(name="work", bufs=2))
        psum = stack.enter_context(tc.psum_pool(name="psum", bufs=2))

        mk_bf = keep.tile([P, HALVES * COMP, I_HALF, COMP], BF16, align_bytes=4096)

        def place(h, c):
            return COMP - 1 - c if h == 0 else COMP + c

        shared = keep.tile([P, TILES * N_OUT], F32, align_bytes=4096)
        results = shared[:].rearrange("p (j n) -> p j n", n=N_OUT)
        z_all = shared[:, TILES * (N_OUT - K) :].rearrange("p (j n) -> p j n", n=K)
        g_all = keep.tile([P, TILES, K], BF16, align_bytes=4096)
        first, count = 0, PAIR
        while first < TILES:
            tiles = slice(first, first + count)
            nc.sync.dma_start(out=z_all[:, tiles, :], in_=z_rows[:, tiles, :])
            if first == 0:
                nc.sync.dma_start(
                    out=mk_bf[:, COMP - 1 : COMP + 1, :, :], in_=W.rearrange("o (h i) e -> o h i e", h=HALVES)
                )
            if first > 0:
                g_tiles = slice(0 if first == PAIR else first, first + count)
                nc.sync.dma_start(out=g_all[:, g_tiles, :], in_=g_rows[:, g_tiles, :])
            first += count
            count = min(first, LOAD_MAX)

        identity = keep.tile([P, P], F32)
        make_identity(nc, identity[:])

        signs = keep.tile([P, COMP, COMP], BF16)
        nc.vector.memset(signs[:], 1.0)
        for c in range(COMP):
            for d in range(COMP):
                if SIGN[c][d] < 0:
                    nc.vector.memset(signs[:, c, d : d + 1], -1.0)
        for h in range(HALVES):
            w_pairs = mk_bf[:, place(h, 0), :, :].rearrange("o i (a b) -> o i a b", b=2)
            for c in range(1, COMP):
                nc.vector.tensor_tensor(
                    out=mk_bf[:, place(h, c), :, :].rearrange("o i (a b) -> o i a b", b=2),
                    in0=w_pairs[:, :, :: (-1 if c & 2 else 1), :: (-1 if c & 1 else 1)],
                    in1=signs[:, c, :]
                    .rearrange("o (a b) -> o a b", b=2)
                    .unsqueeze(1)
                    .to_broadcast([P, I_HALF, 2, 2]),
                    op=ALU.mult,
                )
        mk_codes = keep.tile([P, N_OUT], U32, align_bytes=64)
        mk_scales = keep.tile([P, N_OUT], U8, align_bytes=64)

        def quantise_mk():
            nc.vector.quantize_mx(
                out=mk_codes[:].bitcast(E4M3_X4),
                scales=mk_scales[:],
                in_=mk_bf[:].rearrange("o m i d -> o (m i d)"),
            )

        tanhs, squares, turneds, groupeds, operands, products = {}, {}, {}, {}, {}, {}
        group_first = {}
        first_step = 0
        for size in STORE_GROUPS:
            group_first[first_step + size - 1] = first_step
            first_step += size

        def tanh(k):
            t = work.tile([P, PAIR * K], F32)
            nc.scalar.activation(
                out=t[:],
                in_=z_all[:, PAIR * k : PAIR * (k + 1), :].rearrange("p j n -> p (j n)"),
                func=ACT.Tanh,
            )
            tanhs[k] = t

        def gp_helps(k):
            return 3 <= k < STEPS

        own = PAIR * K - GP_COLS
        square_tile = keep.tile([P, own + GP_COLS + own], F32)

        def square_run(k):
            return square_tile[:, : PAIR * K] if k % 2 == 0 else square_tile[:, own:]

        def gp_columns(k):
            return slice(own, PAIR * K) if k % 2 == 0 else slice(0, GP_COLS)

        def square(k):
            mine = slice(0, PAIR * K)
            if gp_helps(k):
                mine = slice(0, own) if k % 2 == 0 else slice(GP_COLS, PAIR * K)
                squares[k] = square_run(k)
            else:
                t2 = work.tile([P, PAIR * K], F32, bufs=3)
                squares[k] = t2[:]
            nc.scalar.activation(out=squares[k][:, mine], in_=tanhs[k][:, mine], func=ACT.Square)

        def gp_square(k):
            t = tanhs[k][:, gp_columns(k)]
            nc.gpsimd.tensor_tensor(out=square_run(k)[:, gp_columns(k)], in0=t, in1=t, op=ALU.mult)

        def gradient_and_turn(k):
            minus_dz = work.tile([P, PAIR * K], BF16)
            nc.vector.scalar_tensor_tensor(
                out=minus_dz[:],
                in0=squares[k],
                scalar=1.0,
                in1=g_all[:, PAIR * k : PAIR * (k + 1), :].rearrange("p j n -> p (j n)"),
                op0=ALU.subtract,
                op1=ALU.mult,
            )
            words = minus_dz[:].bitcast(F32).rearrange("p (j o u) -> p j u o", j=PAIR, u=2)
            turned = psum.tile([P, 2, PAIR * P], F32)
            for j in range(PAIR):
                for u in range(2):
                    nc.tensor.transpose(
                        out=turned[:, u, j * P : (j + 1) * P], in_=words[:, j, u, :], identity=identity[:]
                    )
            turneds[k] = turned

        def regroup(k):
            grouped = work.tile([P, PAIR * P * COMP], BF16, align_bytes=64)
            nc.vector.tensor_copy(
                out=grouped[:].bitcast(F32).rearrange("o (b u) -> o b u", u=2),
                in_=turneds[k][:].rearrange("o u b -> o b u"),
            )
            groupeds[k] = grouped

        def quantise(k):
            dz_codes = work.tile([P, PAIR * P], U32, bufs=3, align_bytes=64)
            dz_scales = work.tile([P, PAIR * P], U8, bufs=3, align_bytes=64)
            nc.vector.quantize_mx(out=dz_codes[:].bitcast(E5M2_X4), scales=dz_scales[:], in_=groupeds[k][:])
            operands[k] = (dz_codes, dz_scales)

        def multiply(k):
            dz_codes, dz_scales = operands[k]
            for j in range(PAIR):
                rows = slice(j * P, (j + 1) * P)
                for h in reversed(range(HALVES)):
                    cols = slice(h * BANK, (h + 1) * BANK)
                    product = psum.tile([P, BANK], F32, bufs=6)
                    nc.tensor.matmul_mx(
                        out=product[:],
                        lhsT=dz_codes[:, rows].bitcast(E5M2_X4),
                        lhsT_scale=dz_scales[:, rows],
                        rhs=mk_codes[:, cols].bitcast(E4M3_X4),
                        rhs_scale=mk_scales[:, cols],
                        start=True,
                        stop=True,
                    )
                    products[(k, j, h)] = product

        def leave_psum(k, j):
            vector_helps = k < STEPS - 3 or k == STEPS - 1 or (k == STEPS - 2 and j == PAIR - 1)
            vector_alone = False
            for h in reversed(range(HALVES)):
                dest = results[:, PAIR * k + j, h * BANK : (h + 1) * BANK].rearrange(
                    "p (i c) -> p i c", c=COMP
                )
                source = products[(k, j, h)][:].rearrange("p (c i) -> p i c", c=COMP)
                if h == 0:
                    source = source[:, :, ::-1]
                if (h == 0 and vector_helps) or vector_alone:
                    nc.vector.tensor_scalar_mul(out=dest, in0=source, scalar1=-1.0)
                else:
                    nc.scalar.mul(out=dest, in_=source, mul=-1.0)

        def store(first, last):
            tiles = slice(PAIR * first, PAIR * (last + 1))
            nc.sync.dma_start(out=out_rows[:, tiles, :], in_=results[:, tiles, :])

        for r in range(STEPS + 3):
            if 0 <= r - 3:
                multiply(r - 3)
            if r < STEPS:
                tanh(r)
            if 0 <= r - 1 < STEPS:
                gradient_and_turn(r - 1)
            if r == 1:
                quantise_mk()
            if 0 <= r - 2 < STEPS:
                regroup(r - 2)
            if 0 <= r - 3:
                leave_psum(r - 3, 0)
            if r < STEPS and gp_helps(r):
                gp_square(r)
            if r < STEPS:
                square(r)
            if 0 <= r - 2 < STEPS:
                quantise(r - 2)
            if 0 <= r - 3:
                leave_psum(r - 3, 1)
                if r - 3 in group_first:
                    store(group_first[r - 3], r - 3)
